import numpy as np
import ml_dtypes


def mxq(x, axis, fmt="e4m3"):
    dtype, down = {"e4m3": (ml_dtypes.float8_e4m3fn, 7), "e5m2": (ml_dtypes.float8_e5m2, 14)}[fmt]
    v = np.moveaxis(np.asarray(x, np.float32).astype(ml_dtypes.bfloat16).astype(np.float64), axis, -1)
    blocks = v.reshape(v.shape[:-1] + (-1, 32))
    amax = np.abs(blocks).max(-1, keepdims=True)
    byte = np.maximum(np.where(amax > 0, np.frexp(amax)[1] - 1 + 127, 0) - down, 1)
    scale = np.exp2(byte - 127.0)
    codes = (blocks / scale).astype(np.float32).astype(dtype).astype(np.float64)
    return np.moveaxis((codes * scale).reshape(v.shape), -1, axis)


WIDE = False


def mx_kscale(k):
    if not WIDE:
        return np.ones(k)
    levels = np.array([10, -10, 5, -5, 0])
    a = np.random.permutation(np.resize(levels, k // 512 * 4)).reshape(k // 512, 4)
    idx = np.arange(k)
    return np.exp2(a[idx // 512, idx % 128 // 32])


BF16 = ml_dtypes.bfloat16


def bf(x):
    return np.asarray(x, np.float32).astype(BF16)


def f64(x):
    return np.asarray(x).astype(np.float64)


E2M1 = np.array([0.0, 0.5, 1.0, 1.5, 2.0, 3.0, 4.0, 6.0, -0.0, -0.5, -1.0, -1.5, -2.0, -3.0, -4.0, -6.0])


def pack_weight(w, fmt):
    k, n = w.shape
    w = f64(bf(w)).reshape(k // 32, 32, n)
    amax = np.abs(w).max(1)
    if fmt == "e4m3":
        byte = np.frexp(amax)[1] - 1 + 127 - 7
    else:
        mant, ex = np.frexp(amax / 6.0)
        byte = np.where(mant > 0.5, ex, ex - 1) + 127
    byte = np.clip(np.where(amax > 0, byte, 1), 1, 254)
    scaled = (w * np.exp2(127.0 - byte)[:, None, :]).reshape(k, n).astype(np.float32)
    by_word = np.ascontiguousarray(scaled.reshape(k // 512, 128, 4, n).transpose(0, 1, 3, 2))
    if fmt == "e4m3":
        words = by_word.astype(ml_dtypes.float8_e4m3fn).view(np.uint8)
    else:
        c = by_word.astype(ml_dtypes.float4_e2m1fn).view(np.uint8) & 0xF
        words = c[..., 0::2] | (c[..., 1::2] << 4)
    return np.ascontiguousarray(words), np.ascontiguousarray(byte.astype(np.uint8).reshape(k // 512, 16, n))


def unpack_weight(words, scales, fmt):
    g, p, n, _ = words.shape
    if fmt == "e4m3":
        vals = np.ascontiguousarray(words).view(ml_dtypes.float8_e4m3fn).astype(np.float64)
    else:
        nib = np.empty((g, p, n, 4), np.uint8)
        nib[..., 0::2] = words & 0xF
        nib[..., 1::2] = words >> 4
        vals = E2M1[nib]
    vals = vals * np.repeat(np.exp2(scales.astype(np.float64) - 127.0), 8, axis=1)[..., None]
    return vals.transpose(0, 1, 3, 2).reshape(g * 512, n)


BS, H, XDIM = 128, 1024, 2560
IN = XDIM + 2 * H
FMT = "e4m3"


def sigmoid(v):
    return 1.0 / (1.0 + np.exp(-v))


def setup_inputs():
    s = mx_kscale(IN)
    c = 1.0 / np.sqrt(IN)

    def draw_w():
        return pack_weight((np.random.standard_normal((H, IN)) * c / s[None, :]).T, FMT)

    def draw_b():
        return bf(np.random.standard_normal(H) * 0.3)

    input_x = bf(np.random.standard_normal((BS, XDIM)) * s[:XDIM])
    previous_time = bf(np.random.standard_normal((BS, H)) * s[XDIM:XDIM + H])
    previous_layer = bf(np.random.standard_normal((BS, H)) * s[XDIM + H:])
    old_state = bf(np.random.standard_normal((BS, H)) * 0.5)
    wi_words, wi_scales = draw_w()
    b_i = draw_b()
    wf_words, wf_scales = draw_w()
    b_f = draw_b()
    wo_words, wo_scales = draw_w()
    b_o = draw_b()
    ws_words, ws_scales = draw_w()
    b_s = draw_b()
    return {
        "input_x": input_x,
        "previous_time": previous_time,
        "previous_layer": previous_layer,
        "old_state": old_state,
        "Wi_words": wi_words, "Wi_scales": wi_scales, "bi": b_i,
        "Wf_words": wf_words, "Wf_scales": wf_scales, "bf": b_f,
        "Wo_words": wo_words, "Wo_scales": wo_scales, "bo": b_o,
        "Ws_words": ws_words, "Ws_scales": ws_scales, "bs_state": b_s,
    }


def reference(input_x, previous_time, previous_layer, old_state, Wi_words, Wi_scales, bi, Wf_words, Wf_scales, bf, Wo_words, Wo_scales, bo, Ws_words, Ws_scales, bs_state):
    z = np.concatenate([f64(input_x), f64(previous_time), f64(previous_layer)], axis=1)
    W_all_t = np.concatenate([
        unpack_weight(Wi_words, Wi_scales, FMT),
        unpack_weight(Wf_words, Wf_scales, FMT),
        unpack_weight(Wo_words, Wo_scales, FMT),
        unpack_weight(Ws_words, Ws_scales, FMT),
    ], axis=1)
    b_all = np.concatenate([f64(bi), f64(bf), f64(bo), f64(bs_state)], axis=0)
    proj = (mxq(z, 1, "e4m3") @ W_all_t) + b_all
    gi, gf, go, gs = np.split(proj, 4, axis=1)
    input_gate = sigmoid(gi)
    forget_gate = sigmoid(gf)
    output_gate = sigmoid(go)
    new_state = forget_gate * f64(old_state) + input_gate * np.tanh(gs)
    new_hidden = output_gate * np.tanh(new_state)
    return new_hidden

@@ -1,0 +1,192 @@
+from contextlib import ExitStack
+
+import concourse.mybir as mybir
+from concourse.masks import make_identity
+
+F32 = mybir.dt.float32
+BF16 = mybir.dt.bfloat16
+I32 = mybir.dt.int32
+U32 = mybir.dt.uint32
+U8 = mybir.dt.uint8
+FP8X4 = mybir.dt.float8_e4m3fn_x4
+ACT = mybir.ActivationFunctionType
+ALU = mybir.AluOpType
+
+P = 128
+H = 1024
+XDIM = 2560
+K = XDIM + 2 * H
+G = K // 512
+NB = 512
+FLOPS = 2 * P * K * 4 * H
+
+
+def tile_rnn_unit_w_kernel(
+    tc,
+    input_x, previous_time, previous_layer, old_state,
+    Wi_words, Wi_scales, bi,
+    Wf_words, Wf_scales, bf,
+    Wo_words, Wo_scales, bo,
+    Ws_words, Ws_scales, bs_state,
+    out,
+):
+    nc = tc.nc
+    words = [Wf_words, Wi_words, Ws_words, Wo_words]
+    scales = [Wf_scales, Wi_scales, Ws_scales, Wo_scales]
+    biases = [bf, bi, bs_state, bo]
+    funcs = [ACT.Sigmoid, ACT.Sigmoid, ACT.Tanh, ACT.Sigmoid]
+    chunks = [(0, 3), (3, 6), (6, 9)]
+    last_chunks = [(0, 3), (3, 6), (6, 8)]
+
+    with ExitStack() as ctx:
+        keep = ctx.enter_context(tc.tile_pool(name="keep", bufs=1))
+        psum = ctx.enter_context(tc.psum_pool(name="psum", bufs=4))
+        ctx.enter_context(tc.manual_schedule())
+
+        z_sb = keep.tile([P, K], BF16, align_bytes=64)
+        ident = keep.tile([P, P], F32)
+        grouped = keep.tile([P, G * 512], BF16, align_bytes=64)
+        zc = keep.tile([P, G * P], U32, align_bytes=64)
+        zs = keep.tile([P, G * P], U8, align_bytes=64)
+        w_sb = [keep.tile([P, G, 4 * H], U8, align_bytes=64, name="w_sb%d" % w) for w in range(4)]
+        planes = [keep.tile([P, 3, H], U8, align_bytes=64, name="planes%d" % w) for w in range(4)]
+        brow = keep.tile([P, 4 * H], BF16)
+        ones = keep.tile([P, P], BF16)
+        bias_bc = keep.tile([P, 4 * H], BF16)
+        old = keep.tile([P, H], BF16)
+        pre = [keep.tile([P, H], F32, name="pre%d" % w) for w in range(4)]
+
+        for w in range(4):
+            nc.vector.memset(planes[w][:].bitcast(I32), 0)
+        nc.vector.memset(brow[:].bitcast(I32), 0)
+        nc.vector.memset(ones[:], 1.0)
+        make_identity(nc, ident[:])
+
+        nc.sync.dma_start(out=z_sb[:, 0:XDIM], in_=input_x)
+        nc.sync.dma_start(out=z_sb[:, XDIM:XDIM + H], in_=previous_time)
+        nc.sync.dma_start(out=z_sb[:, XDIM + H:K], in_=previous_layer)
+        for w in range(4):
+            nc.scalar.dma_start(
+                out=brow[0:1, w * H:(w + 1) * H],
+                in_=biases[w].rearrange("(o n) -> o n", o=1),
+            )
+
+        def load_scales(w, a):
+            for q in range(4):
+                if a < 2:
+                    nc.sync.dma_start(
+                        out=planes[w][32 * q:32 * q + 16, a, :].bitcast(I32),
+                        in_=scales[w][4 * a:4 * a + 4, 4 * q:4 * q + 4, :].bitcast(I32),
+                    )
+                else:
+                    nc.sync.dma_start(
+                        out=planes[w][32 * q:32 * q + 4, a, :].bitcast(I32),
+                        in_=scales[w][8, 4 * q:4 * q + 4, :].bitcast(I32),
+                    )
+
+        def load_words(w, g0, g1):
+            nc.sync.dma_start(
+                out=w_sb[w][:, g0:g1, :].bitcast(I32),
+                in_=words[w][g0:g1].rearrange("g p n t -> p g (n t)").bitcast(I32),
+            )
+
+        for w in range(4):
+            for a, (g0, g1) in enumerate(chunks if w < 3 else last_chunks):
+                load_scales(w, a)
+                load_words(w, g0, g1)
+                if w == 0 and a == 1:
+                    nc.sync.dma_start(out=old[:], in_=old_state)
+        for h in range(2):
+            nc.sync.dma_start(
+                out=w_sb[3][:, 8, 2048 * h:2048 * (h + 1)].bitcast(I32),
+                in_=words[3][8].rearrange("p n t -> p (n t)")[:, 2048 * h:2048 * (h + 1)].bitcast(I32),
+            )
+
+        zw = z_sb[:].bitcast(F32)
+        grouped_w = grouped[:].bitcast(F32).rearrange("p (g b u) -> p g b u", g=G, b=P, u=2)
+        tps = []
+
+        def transposes(j):
+            ng = min(2, G - 2 * j)
+            tp = psum.tile([P, ng, 2, P], F32, tag="tp", name="tp%d" % j)
+            for gg in range(ng):
+                g = 2 * j + gg
+                for u in range(2):
+                    nc.tensor.transpose(tp[:, gg, u, :], zw[:, 256 * g + u:256 * (g + 1):2], ident[:])
+            tps.append(tp)
+
+        def copy_out(j, eng_copy):
+            ng = min(2, G - 2 * j)
+            eng_copy(
+                out=grouped_w[:, 2 * j:2 * j + ng, :, :],
+                in_=tps[j][:].rearrange("p g u b -> p g b u"),
+            )
+
+        def quantise(j):
+            ng = min(2, G - 2 * j)
+            nc.vector.quantize_mx(
+                out=zc[:, 256 * j:256 * j + P * ng].bitcast(FP8X4),
+                scales=zs[:, 256 * j:256 * j + P * ng],
+                in_=grouped[:, 1024 * j:1024 * j + 512 * ng],
+            )
+
+        for j in range(4):
+            transposes(j)
+        copy_out(0, nc.vector.tensor_copy)
+        transposes(4)
+        copy_out(1, nc.scalar.copy)
+        copy_out(2, nc.vector.tensor_copy)
+        copy_out(3, nc.scalar.copy)
+        quantise(0)
+        quantise(1)
+        copy_out(4, nc.vector.tensor_copy)
+        quantise(2)
+        quantise(3)
+        quantise(4)
+
+        for c in range(8):
+            bp = psum.tile([P, NB], F32, tag="tp", name="bp%d" % c)
+            nc.tensor.matmul(out=bp[:], lhsT=ones[:], rhs=brow[:, NB * c:NB * (c + 1)], start=True, stop=True)
+            if c % 2 == 0:
+                nc.scalar.copy(out=bias_bc[:, NB * c:NB * (c + 1)], in_=bp[:])
+            else:
+                nc.vector.tensor_copy(out=bias_bc[:, NB * c:NB * (c + 1)], in_=bp[:])
+
+        def mx_pass(w, acc, g, h):
+            a, k = g // 4, g % 4
+            nc.tensor.matmul_mx(
+                out=acc[:],
+                lhsT=zc[:, P * g:P * (g + 1)].bitcast(FP8X4),
+                lhsT_scale=zs[:, P * g:P * (g + 1)],
+                rhs=w_sb[w][:, g, 2048 * h:2048 * (h + 1)].bitcast(FP8X4),
+                rhs_scale=planes[w][4 * k:P, a, NB * h:NB * (h + 1)],
+                start=(g == 0),
+                stop=(g == G - 1),
+            )
+
+        def gate(w, acc, h):
+            cols = slice(NB * h, NB * (h + 1))
+            nc.vector.tensor_tensor(
+                out=pre[w][:, cols], in0=acc[:],
+                in1=bias_bc[:, w * H + NB * h:w * H + NB * (h + 1)], op=ALU.add,
+            )
+            nc.scalar.activation(out=pre[w][:, cols], in_=pre[w][:, cols], func=funcs[w])
+
+        for w in range(4):
+            accs = [psum.tile([P, NB], F32, tag="acc", name="acc%d_%d" % (w, h)) for h in range(2)]
+            for g in range(G - 1):
+                for h in range(2):
+                    mx_pass(w, accs[h], g, h)
+            for h in range(2):
+                cols = slice(NB * h, NB * (h + 1))
+                mx_pass(w, accs[h], G - 1, h)
+                gate(w, accs[h], h)
+                if w == 0:
+                    nc.vector.tensor_tensor(out=pre[0][:, cols], in0=pre[0][:, cols], in1=old[:, cols], op=ALU.mult)
+                if w == 2:
+                    nc.vector.tensor_tensor(out=pre[1][:, cols], in0=pre[1][:, cols], in1=pre[2][:, cols], op=ALU.mult)
+                    nc.vector.tensor_tensor(out=pre[0][:, cols], in0=pre[0][:, cols], in1=pre[1][:, cols], op=ALU.add)
+                    nc.scalar.activation(out=pre[0][:, cols], in_=pre[0][:, cols], func=ACT.Tanh)
+                if w == 3:
+                    nc.vector.tensor_tensor(out=pre[3][:, cols], in0=pre[3][:, cols], in1=pre[0][:, cols], op=ALU.mult)
+                    nc.sync.dma_start(out=out[:, cols], in_=pre[3][:, cols])

@@ -74,14 +74,14 @@ def tile_rnn_unit_w_kernel(
         def load_scales(w, a):
             for q in range(4):
                 if a < 2:
-                    nc.sync.dma_start(
-                        out=planes[w][32 * q:32 * q + 16, a, :].bitcast(I32),
-                        in_=scales[w][4 * a:4 * a + 4, 4 * q:4 * q + 4, :].bitcast(I32),
+                    nc.gpsimd.dma_start(
+                        out=planes[w][32 * q:32 * q + 16, a, :].bitcast(F32),
+                        in_=scales[w][4 * a:4 * a + 4, 4 * q:4 * q + 4, :].bitcast(F32),
                     )
                 else:
-                    nc.sync.dma_start(
-                        out=planes[w][32 * q:32 * q + 4, a, :].bitcast(I32),
-                        in_=scales[w][8, 4 * q:4 * q + 4, :].bitcast(I32),
+                    nc.gpsimd.dma_start(
+                        out=planes[w][32 * q:32 * q + 4, a, :].bitcast(F32),
+                        in_=scales[w][8, 4 * q:4 * q + 4, :].bitcast(F32),
                     )
 
         def load_words(w, g0, g1):

@@ -36,7 +36,8 @@ def tile_rnn_unit_w_kernel(
     biases = [bf, bi, bs_state, bo]
     funcs = [ACT.Sigmoid, ACT.Sigmoid, ACT.Tanh, ACT.Sigmoid]
     chunks = [(0, 3), (3, 6), (6, 9)]
-    last_chunks = [(0, 3), (3, 6), (6, 8)]
+    GA = 6
+    NQ = 256
 
     with ExitStack() as ctx:
         keep = ctx.enter_context(tc.tile_pool(name="keep", bufs=1))
@@ -79,9 +80,9 @@ def tile_rnn_unit_w_kernel(
                         in_=scales[w][4 * a:4 * a + 4, 4 * q:4 * q + 4, :].bitcast(F32),
                     )
                 else:
-                    nc.gpsimd.dma_start(
-                        out=planes[w][32 * q:32 * q + 4, a, :].bitcast(F32),
-                        in_=scales[w][8, 4 * q:4 * q + 4, :].bitcast(F32),
+                    nc.sync.dma_start(
+                        out=planes[w][32 * q:32 * q + 4, a, :].bitcast(I32),
+                        in_=scales[w][8, 4 * q:4 * q + 4, :].bitcast(I32),
                     )
 
         def load_words(w, g0, g1):
@@ -91,15 +92,17 @@ def tile_rnn_unit_w_kernel(
             )
 
         for w in range(4):
-            for a, (g0, g1) in enumerate(chunks if w < 3 else last_chunks):
+            for a in range(3):
                 load_scales(w, a)
-                load_words(w, g0, g1)
-                if w == 0 and a == 1:
+            for g0, g1 in chunks:
+                if w < 3 or g1 <= GA:
+                    load_words(w, g0, g1)
+                if w == 0 and g0 == 3:
                     nc.sync.dma_start(out=old[:], in_=old_state)
-        for h in range(2):
+        for c in range(4):
             nc.sync.dma_start(
-                out=w_sb[3][:, 8, 2048 * h:2048 * (h + 1)].bitcast(I32),
-                in_=words[3][8].rearrange("p n t -> p (n t)")[:, 2048 * h:2048 * (h + 1)].bitcast(I32),
+                out=w_sb[3][:, GA:G, 4 * NQ * c:4 * NQ * (c + 1)].bitcast(I32),
+                in_=words[3][GA:G].rearrange("g p n t -> p g (n t)")[:, :, 4 * NQ * c:4 * NQ * (c + 1)].bitcast(I32),
             )
 
         zw = z_sb[:].bitcast(F32)
@@ -152,41 +155,61 @@ def tile_rnn_unit_w_kernel(
             else:
                 nc.vector.tensor_copy(out=bias_bc[:, NB * c:NB * (c + 1)], in_=bp[:])
 
-        def mx_pass(w, acc, g, h):
+        def mx_pass(w, acc, g, c0, n, start, stop):
             a, k = g // 4, g % 4
             nc.tensor.matmul_mx(
                 out=acc[:],
                 lhsT=zc[:, P * g:P * (g + 1)].bitcast(FP8X4),
                 lhsT_scale=zs[:, P * g:P * (g + 1)],
-                rhs=w_sb[w][:, g, 2048 * h:2048 * (h + 1)].bitcast(FP8X4),
-                rhs_scale=planes[w][4 * k:P, a, NB * h:NB * (h + 1)],
-                start=(g == 0),
-                stop=(g == G - 1),
+                rhs=w_sb[w][:, g, 4 * c0:4 * (c0 + n)].bitcast(FP8X4),
+                rhs_scale=planes[w][4 * k:P, a, c0:c0 + n],
+                start=start,
+                stop=stop,
             )
 
-        def gate(w, acc, h):
-            cols = slice(NB * h, NB * (h + 1))
-            nc.vector.tensor_tensor(
-                out=pre[w][:, cols], in0=acc[:],
-                in1=bias_bc[:, w * H + NB * h:w * H + NB * (h + 1)], op=ALU.add,
-            )
-            nc.scalar.activation(out=pre[w][:, cols], in_=pre[w][:, cols], func=funcs[w])
+        halves = [slice(NB * h, NB * (h + 1)) for h in range(2)]
 
-        for w in range(4):
-            accs = [psum.tile([P, NB], F32, tag="acc", name="acc%d_%d" % (w, h)) for h in range(2)]
-            for g in range(G - 1):
-                for h in range(2):
-                    mx_pass(w, accs[h], g, h)
+        def add_bias(w, accs):
             for h in range(2):
-                cols = slice(NB * h, NB * (h + 1))
-                mx_pass(w, accs[h], G - 1, h)
-                gate(w, accs[h], h)
+                nc.vector.tensor_tensor(
+                    out=pre[w][:, halves[h]], in0=accs[h][:],
+                    in1=bias_bc[:, w * H + NB * h:w * H + NB * (h + 1)], op=ALU.add,
+                )
+
+        for w in range(3):
+            accs = [psum.tile([P, NB], F32, tag="acc", name="acc%d_%d" % (w, h)) for h in range(2)]
+            for g in range(G):
+                for h in range(2):
+                    mx_pass(w, accs[h], g, NB * h, NB, g == 0, g == G - 1)
+            add_bias(w, accs)
+            for cols in halves:
+                nc.scalar.activation(out=pre[w][:, cols], in_=pre[w][:, cols], func=funcs[w])
+            for cols in halves:
                 if w == 0:
                     nc.vector.tensor_tensor(out=pre[0][:, cols], in0=pre[0][:, cols], in1=old[:, cols], op=ALU.mult)
                 if w == 2:
                     nc.vector.tensor_tensor(out=pre[1][:, cols], in0=pre[1][:, cols], in1=pre[2][:, cols], op=ALU.mult)
                     nc.vector.tensor_tensor(out=pre[0][:, cols], in0=pre[0][:, cols], in1=pre[1][:, cols], op=ALU.add)
                     nc.scalar.activation(out=pre[0][:, cols], in_=pre[0][:, cols], func=ACT.Tanh)
-                if w == 3:
-                    nc.vector.tensor_tensor(out=pre[3][:, cols], in0=pre[3][:, cols], in1=pre[0][:, cols], op=ALU.mult)
-                    nc.sync.dma_start(out=out[:, cols], in_=pre[3][:, cols])
+
+        accs = [psum.tile([P, NB], F32, tag="acc", name="acc3_%d" % h) for h in range(2)]
+        for g in range(GA):
+            for h in range(2):
+                mx_pass(3, accs[h], g, NB * h, NB, g == 0, g == GA - 1)
+        add_bias(3, accs)
+
+        def finish(c):
+            cols = slice(NQ * c, NQ * (c + 1))
+            nc.vector.tensor_tensor(out=pre[3][:, cols], in0=pre[3][:, cols], in1=pre[0][:, cols], op=ALU.mult)
+            nc.sync.dma_start(out=out[:, cols], in_=pre[3][:, cols])
+
+        for c in range(4):
+            cols = slice(NQ * c, NQ * (c + 1))
+            rest = psum.tile([P, NQ], F32, tag="tp", name="rest%d" % c)
+            for g in range(GA, G):
+                mx_pass(3, rest, g, NQ * c, NQ, g == GA, g == G - 1)
+            nc.vector.tensor_tensor(out=pre[3][:, cols], in0=rest[:], in1=pre[3][:, cols], op=ALU.add)
+            nc.scalar.activation(out=pre[3][:, cols], in_=pre[3][:, cols], func=ACT.Sigmoid)
+            if c > 0:
+                finish(c - 1)
+        finish(3)

@@ -35,7 +35,7 @@ def tile_rnn_unit_w_kernel(
     scales = [Wf_scales, Wi_scales, Ws_scales, Wo_scales]
     biases = [bf, bi, bs_state, bo]
     funcs = [ACT.Sigmoid, ACT.Sigmoid, ACT.Tanh, ACT.Sigmoid]
-    chunks = [(0, 3), (3, 6), (6, 9)]
+    chunks = [(g, g + 1) for g in range(G)]
     GA = 6
     NQ = 256
 
@@ -81,7 +81,7 @@ def tile_rnn_unit_w_kernel(
                     )
                 else:
                     nc.sync.dma_start(
-                        out=planes[w][32 * q:32 * q + 4, a, :].bitcast(I32),
+                        out=planes[w][32 * q + 4 * w:32 * q + 4 * w + 4, a, :].bitcast(I32),
                         in_=scales[w][8, 4 * q:4 * q + 4, :].bitcast(I32),
                     )
 
@@ -156,7 +156,7 @@ def tile_rnn_unit_w_kernel(
                 nc.vector.tensor_copy(out=bias_bc[:, NB * c:NB * (c + 1)], in_=bp[:])
 
         def mx_pass(w, acc, g, c0, n, start, stop):
-            a, k = g // 4, g % 4
+            a, k = (g // 4, g % 4) if g < 8 else (2, w)
             nc.tensor.matmul_mx(
                 out=acc[:],
                 lhsT=zc[:, P * g:P * (g + 1)].bitcast(FP8X4),

@@ -35,7 +35,7 @@ def tile_rnn_unit_w_kernel(
     scales = [Wf_scales, Wi_scales, Ws_scales, Wo_scales]
     biases = [bf, bi, bs_state, bo]
     funcs = [ACT.Sigmoid, ACT.Sigmoid, ACT.Tanh, ACT.Sigmoid]
-    chunks = [(g, g + 1) for g in range(G)]
+    chunks = [(0, 3), (3, 6), (6, 9)]
     GA = 6
     NQ = 256
 
@@ -99,10 +99,10 @@ def tile_rnn_unit_w_kernel(
                     load_words(w, g0, g1)
                 if w == 0 and g0 == 3:
                     nc.sync.dma_start(out=old[:], in_=old_state)
-        for c in range(4):
+        for c, g0, g1 in [(0, GA, G), (1, GA, G), (2, GA, G), (3, GA, G - 1), (3, G - 1, G)]:
             nc.sync.dma_start(
-                out=w_sb[3][:, GA:G, 4 * NQ * c:4 * NQ * (c + 1)].bitcast(I32),
-                in_=words[3][GA:G].rearrange("g p n t -> p g (n t)")[:, :, 4 * NQ * c:4 * NQ * (c + 1)].bitcast(I32),
+                out=w_sb[3][:, g0:g1, 4 * NQ * c:4 * NQ * (c + 1)].bitcast(I32),
+                in_=words[3][g0:g1].rearrange("g p n t -> p g (n t)")[:, :, 4 * NQ * c:4 * NQ * (c + 1)].bitcast(I32),
             )
 
         zw = z_sb[:].bitcast(F32)

@@ -95,8 +95,11 @@ def tile_rnn_unit_w_kernel(
             for a in range(3):
                 load_scales(w, a)
             for g0, g1 in chunks:
-                if w < 3 or g1 <= GA:
+                if w < 3:
                     load_words(w, g0, g1)
+                elif g1 <= GA:
+                    for g in range(g0, g1):
+                        load_words(w, g, g + 1)
                 if w == 0 and g0 == 3:
                     nc.sync.dma_start(out=old[:], in_=old_state)
         for c, g0, g1 in [(0, GA, G), (1, GA, G), (2, GA, G), (3, GA, G - 1), (3, G - 1, G)]:
@@ -192,24 +195,24 @@ def tile_rnn_unit_w_kernel(
                     nc.vector.tensor_tensor(out=pre[0][:, cols], in0=pre[0][:, cols], in1=pre[1][:, cols], op=ALU.add)
                     nc.scalar.activation(out=pre[0][:, cols], in_=pre[0][:, cols], func=ACT.Tanh)
 
-        accs = [psum.tile([P, NB], F32, tag="acc", name="acc3_%d" % h) for h in range(2)]
-        for g in range(GA):
-            for h in range(2):
-                mx_pass(3, accs[h], g, NB * h, NB, g == 0, g == GA - 1)
-        add_bias(3, accs)
-
-        def finish(c):
+        def finish(c, eng):
             cols = slice(NQ * c, NQ * (c + 1))
-            nc.vector.tensor_tensor(out=pre[3][:, cols], in0=pre[3][:, cols], in1=pre[0][:, cols], op=ALU.mult)
+            eng.tensor_tensor(out=pre[3][:, cols], in0=pre[3][:, cols], in1=pre[0][:, cols], op=ALU.mult)
             nc.sync.dma_start(out=out[:, cols], in_=pre[3][:, cols])
 
+        rests = [psum.tile([P, NQ], F32, tag="tp", name="rest%d" % c) for c in range(4)]
+        for g in range(GA):
+            for c in range(4):
+                mx_pass(3, rests[c], g, NQ * c, NQ, g == 0, False)
         for c in range(4):
             cols = slice(NQ * c, NQ * (c + 1))
-            rest = psum.tile([P, NQ], F32, tag="tp", name="rest%d" % c)
             for g in range(GA, G):
-                mx_pass(3, rest, g, NQ * c, NQ, g == GA, g == G - 1)
-            nc.vector.tensor_tensor(out=pre[3][:, cols], in0=rest[:], in1=pre[3][:, cols], op=ALU.add)
+                mx_pass(3, rests[c], g, NQ * c, NQ, False, g == G - 1)
+            nc.vector.tensor_tensor(
+                out=pre[3][:, cols], in0=rests[c][:],
+                in1=bias_bc[:, 3 * H + NQ * c:3 * H + NQ * (c + 1)], op=ALU.add,
+            )
             nc.scalar.activation(out=pre[3][:, cols], in_=pre[3][:, cols], func=ACT.Sigmoid)
             if c > 0:
-                finish(c - 1)
-        finish(3)
+                finish(c - 1, nc.vector)
+        finish(3, nc.vector)

@@ -44,18 +44,18 @@ def tile_rnn_unit_w_kernel(
         psum = ctx.enter_context(tc.psum_pool(name="psum", bufs=4))
         ctx.enter_context(tc.manual_schedule())
 
-        z_sb = keep.tile([P, K], BF16, align_bytes=64)
+        z_sb = keep.tile([P, K], BF16, align_bytes=256)
         ident = keep.tile([P, P], F32)
         grouped = keep.tile([P, G * 512], BF16, align_bytes=64)
         zc = keep.tile([P, G * P], U32, align_bytes=64)
         zs = keep.tile([P, G * P], U8, align_bytes=64)
-        w_sb = [keep.tile([P, G, 4 * H], U8, align_bytes=64, name="w_sb%d" % w) for w in range(4)]
-        planes = [keep.tile([P, 3, H], U8, align_bytes=64, name="planes%d" % w) for w in range(4)]
+        w_sb = [keep.tile([P, G, 4 * H], U8, align_bytes=4096, name="w_sb%d" % w) for w in range(4)]
+        planes = [keep.tile([P, 3, H], U8, align_bytes=256, name="planes%d" % w) for w in range(4)]
         brow = keep.tile([P, 4 * H], BF16)
         ones = keep.tile([P, P], BF16)
         bias_bc = keep.tile([P, 4 * H], BF16)
-        old = keep.tile([P, H], BF16)
-        pre = [keep.tile([P, H], F32, name="pre%d" % w) for w in range(4)]
+        old = keep.tile([P, H], BF16, align_bytes=256)
+        pre = [keep.tile([P, H], F32, align_bytes=256, name="pre%d" % w) for w in range(4)]
 
         for w in range(4):
             nc.vector.memset(planes[w][:].bitcast(I32), 0)

from contextlib import ExitStack

import concourse.mybir as mybir
from concourse.masks import make_identity

F32 = mybir.dt.float32
BF16 = mybir.dt.bfloat16
I32 = mybir.dt.int32
U32 = mybir.dt.uint32
U8 = mybir.dt.uint8
FP8X4 = mybir.dt.float8_e4m3fn_x4
ACT = mybir.ActivationFunctionType
ALU = mybir.AluOpType

P = 128
H = 1024
XDIM = 2560
K = XDIM + 2 * H
G = K // 512
NB = 512
FLOPS = 2 * P * K * 4 * H


def tile_rnn_unit_w_kernel(
    tc,
    input_x, previous_time, previous_layer, old_state,
    Wi_words, Wi_scales, bi,
    Wf_words, Wf_scales, bf,
    Wo_words, Wo_scales, bo,
    Ws_words, Ws_scales, bs_state,
    out,
):
    nc = tc.nc
    words = [Wf_words, Wi_words, Ws_words, Wo_words]
    scales = [Wf_scales, Wi_scales, Ws_scales, Wo_scales]
    biases = [bf, bi, bs_state, bo]
    funcs = [ACT.Sigmoid, ACT.Sigmoid, ACT.Tanh, ACT.Sigmoid]
    chunks = [(0, 3), (3, 6), (6, 9)]
    GA = 6
    NQ = 256

    with ExitStack() as ctx:
        keep = ctx.enter_context(tc.tile_pool(name="keep", bufs=1))
        psum = ctx.enter_context(tc.psum_pool(name="psum", bufs=4))
        ctx.enter_context(tc.manual_schedule())

        z_sb = keep.tile([P, K], BF16, align_bytes=256)
        ident = keep.tile([P, P], F32)
        grouped = keep.tile([P, G * 512], BF16, align_bytes=64)
        zc = keep.tile([P, G * P], U32, align_bytes=64)
        zs = keep.tile([P, G * P], U8, align_bytes=64)
        w_sb = [keep.tile([P, G, 4 * H], U8, align_bytes=4096, name="w_sb%d" % w) for w in range(4)]
        planes = [keep.tile([P, 3, H], U8, align_bytes=256, name="planes%d" % w) for w in range(4)]
        brow = keep.tile([P, 4 * H], BF16)
        ones = keep.tile([P, P], BF16)
        bias_bc = keep.tile([P, 4 * H], BF16)
        old = keep.tile([P, H], BF16, align_bytes=256)
        pre = [keep.tile([P, H], F32, align_bytes=256, name="pre%d" % w) for w in range(4)]

        for w in range(4):
            nc.vector.memset(planes[w][:].bitcast(I32), 0)
        nc.vector.memset(brow[:].bitcast(I32), 0)
        nc.vector.memset(ones[:], 1.0)
        make_identity(nc, ident[:])

        nc.sync.dma_start(out=z_sb[:, 0:XDIM], in_=input_x)
        nc.sync.dma_start(out=z_sb[:, XDIM:XDIM + H], in_=previous_time)
        nc.sync.dma_start(out=z_sb[:, XDIM + H:K], in_=previous_layer)
        for w in range(4):
            nc.scalar.dma_start(
                out=brow[0:1, w * H:(w + 1) * H],
                in_=biases[w].rearrange("(o n) -> o n", o=1),
            )

        def load_scales(w, a):
            for q in range(4):
                if a < 2:
                    nc.gpsimd.dma_start(
                        out=planes[w][32 * q:32 * q + 16, a, :].bitcast(F32),
                        in_=scales[w][4 * a:4 * a + 4, 4 * q:4 * q + 4, :].bitcast(F32),
                    )
                else:
                    nc.sync.dma_start(
                        out=planes[w][32 * q + 4 * w:32 * q + 4 * w + 4, a, :].bitcast(I32),
                        in_=scales[w][8, 4 * q:4 * q + 4, :].bitcast(I32),
                    )

        def load_words(w, g0, g1):
            nc.sync.dma_start(
                out=w_sb[w][:, g0:g1, :].bitcast(I32),
                in_=words[w][g0:g1].rearrange("g p n t -> p g (n t)").bitcast(I32),
            )

        for w in range(4):
            for a in range(3):
                load_scales(w, a)
            for g0, g1 in chunks:
                if w < 3:
                    load_words(w, g0, g1)
                elif g1 <= GA:
                    for g in range(g0, g1):
                        load_words(w, g, g + 1)
                if w == 0 and g0 == 3:
                    nc.sync.dma_start(out=old[:], in_=old_state)
        for c, g0, g1 in [(0, GA, G), (1, GA, G), (2, GA, G), (3, GA, G - 1), (3, G - 1, G)]:
            nc.sync.dma_start(
                out=w_sb[3][:, g0:g1, 4 * NQ * c:4 * NQ * (c + 1)].bitcast(I32),
                in_=words[3][g0:g1].rearrange("g p n t -> p g (n t)")[:, :, 4 * NQ * c:4 * NQ * (c + 1)].bitcast(I32),
            )

        zw = z_sb[:].bitcast(F32)
        grouped_w = grouped[:].bitcast(F32).rearrange("p (g b u) -> p g b u", g=G, b=P, u=2)
        tps = []

        def transposes(j):
            ng = min(2, G - 2 * j)
            tp = psum.tile([P, ng, 2, P], F32, tag="tp", name="tp%d" % j)
            for gg in range(ng):
                g = 2 * j + gg
                for u in range(2):
                    nc.tensor.transpose(tp[:, gg, u, :], zw[:, 256 * g + u:256 * (g + 1):2], ident[:])
            tps.append(tp)

        def copy_out(j, eng_copy):
            ng = min(2, G - 2 * j)
            eng_copy(
                out=grouped_w[:, 2 * j:2 * j + ng, :, :],
                in_=tps[j][:].rearrange("p g u b -> p g b u"),
            )

        def quantise(j):
            ng = min(2, G - 2 * j)
            nc.vector.quantize_mx(
                out=zc[:, 256 * j:256 * j + P * ng].bitcast(FP8X4),
                scales=zs[:, 256 * j:256 * j + P * ng],
                in_=grouped[:, 1024 * j:1024 * j + 512 * ng],
            )

        for j in range(4):
            transposes(j)
        copy_out(0, nc.vector.tensor_copy)
        transposes(4)
        copy_out(1, nc.scalar.copy)
        copy_out(2, nc.vector.tensor_copy)
        copy_out(3, nc.scalar.copy)
        quantise(0)
        quantise(1)
        copy_out(4, nc.vector.tensor_copy)
        quantise(2)
        quantise(3)
        quantise(4)

        for c in range(8):
            bp = psum.tile([P, NB], F32, tag="tp", name="bp%d" % c)
            nc.tensor.matmul(out=bp[:], lhsT=ones[:], rhs=brow[:, NB * c:NB * (c + 1)], start=True, stop=True)
            if c % 2 == 0:
                nc.scalar.copy(out=bias_bc[:, NB * c:NB * (c + 1)], in_=bp[:])
            else:
                nc.vector.tensor_copy(out=bias_bc[:, NB * c:NB * (c + 1)], in_=bp[:])

        def mx_pass(w, acc, g, c0, n, start, stop):
            a, k = (g // 4, g % 4) if g < 8 else (2, w)
            nc.tensor.matmul_mx(
                out=acc[:],
                lhsT=zc[:, P * g:P * (g + 1)].bitcast(FP8X4),
                lhsT_scale=zs[:, P * g:P * (g + 1)],
                rhs=w_sb[w][:, g, 4 * c0:4 * (c0 + n)].bitcast(FP8X4),
                rhs_scale=planes[w][4 * k:P, a, c0:c0 + n],
                start=start,
                stop=stop,
            )

        halves = [slice(NB * h, NB * (h + 1)) for h in range(2)]

        def add_bias(w, accs):
            for h in range(2):
                nc.vector.tensor_tensor(
                    out=pre[w][:, halves[h]], in0=accs[h][:],
                    in1=bias_bc[:, w * H + NB * h:w * H + NB * (h + 1)], op=ALU.add,
                )

        for w in range(3):
            accs = [psum.tile([P, NB], F32, tag="acc", name="acc%d_%d" % (w, h)) for h in range(2)]
            for g in range(G):
                for h in range(2):
                    mx_pass(w, accs[h], g, NB * h, NB, g == 0, g == G - 1)
            add_bias(w, accs)
            for cols in halves:
                nc.scalar.activation(out=pre[w][:, cols], in_=pre[w][:, cols], func=funcs[w])
            for cols in halves:
                if w == 0:
                    nc.vector.tensor_tensor(out=pre[0][:, cols], in0=pre[0][:, cols], in1=old[:, cols], op=ALU.mult)
                if w == 2:
                    nc.vector.tensor_tensor(out=pre[1][:, cols], in0=pre[1][:, cols], in1=pre[2][:, cols], op=ALU.mult)
                    nc.vector.tensor_tensor(out=pre[0][:, cols], in0=pre[0][:, cols], in1=pre[1][:, cols], op=ALU.add)
                    nc.scalar.activation(out=pre[0][:, cols], in_=pre[0][:, cols], func=ACT.Tanh)

        def finish(c, eng):
            cols = slice(NQ * c, NQ * (c + 1))
            eng.tensor_tensor(out=pre[3][:, cols], in0=pre[3][:, cols], in1=pre[0][:, cols], op=ALU.mult)
            nc.sync.dma_start(out=out[:, cols], in_=pre[3][:, cols])

        rests = [psum.tile([P, NQ], F32, tag="tp", name="rest%d" % c) for c in range(4)]
        for g in range(GA):
            for c in range(4):
                mx_pass(3, rests[c], g, NQ * c, NQ, g == 0, False)
        for c in range(4):
            cols = slice(NQ * c, NQ * (c + 1))
            for g in range(GA, G):
                mx_pass(3, rests[c], g, NQ * c, NQ, False, g == G - 1)
            nc.vector.tensor_tensor(
                out=pre[3][:, cols], in0=rests[c][:],
                in1=bias_bc[:, 3 * H + NQ * c:3 * H + NQ * (c + 1)], op=ALU.add,
            )
            nc.scalar.activation(out=pre[3][:, cols], in_=pre[3][:, cols], func=ACT.Sigmoid)
            if c > 0:
                finish(c - 1, nc.vector)
        finish(3, nc.vector)
